import numpy as np
import ml_dtypes


def mxq(x, axis, fmt="e4m3"):
    dtype, down = {"e4m3": (ml_dtypes.float8_e4m3fn, 7), "e5m2": (ml_dtypes.float8_e5m2, 14)}[fmt]
    v = np.moveaxis(np.asarray(x, np.float32).astype(ml_dtypes.bfloat16).astype(np.float64), axis, -1)
    blocks = v.reshape(v.shape[:-1] + (-1, 32))
    amax = np.abs(blocks).max(-1, keepdims=True)
    byte = np.maximum(np.where(amax > 0, np.frexp(amax)[1] - 1 + 127, 0) - down, 1)
    scale = np.exp2(byte - 127.0)
    codes = (blocks / scale).astype(np.float32).astype(dtype).astype(np.float64)
    return np.moveaxis((codes * scale).reshape(v.shape), -1, axis)


WIDE = False


def mx_kscale(k):
    if not WIDE:
        return np.ones(k)
    levels = np.array([10, -10, 5, -5, 0])
    a = np.random.permutation(np.resize(levels, k // 512 * 4)).reshape(k // 512, 4)
    idx = np.arange(k)
    return np.exp2(a[idx // 512, idx % 128 // 32])


BF16 = ml_dtypes.bfloat16


def bf(x):
    return np.asarray(x, np.float32).astype(BF16)


def f64(x):
    return np.asarray(x).astype(np.float64)


B, S, H, HD = 2, 1024, 8, 128
D = H * HD


def silu(x):
    e = np.exp(-np.abs(x))
    return x * np.where(x >= 0.0, 1.0, e) / (1.0 + e)


def split_heads(x):
    return x.reshape(B, S, H, HD).transpose(0, 2, 1, 3)


def setup_inputs():
    s = mx_kscale(S)
    c = (s / s.min())[None, :, None]
    return {"v": bf(np.random.standard_normal((B, S, D)) * 4.0 / np.sqrt(S) / c),
            "k": bf(np.random.standard_normal((B, S, D)) * 1.2 / HD ** 0.25 * c),
            "q": bf(np.random.standard_normal((B, S, D)) * 1.2 / HD ** 0.25)}


def reference(v, k, q):
    qh = split_heads(f64(q))
    kh = split_heads(f64(k))
    vh = split_heads(f64(v))
    scores = qh @ kh.transpose(0, 1, 3, 2)
    p = silu(scores)
    av = mxq(p, 3, "e4m3") @ mxq(vh, 2, "e4m3")
    return av.transpose(0, 2, 1, 3).reshape(B, S, D)

@@ -1,0 +1,211 @@
+from contextlib import ExitStack
+
+import concourse.mybir as mybir
+from concourse.masks import make_identity
+
+B, S, H, HD = 2, 1024, 8, 128
+D = H * HD
+FLOPS = 2 * 2 * B * H * S * S * HD
+
+P = 128
+PACK = 4
+G = S // (P * PACK)
+NJ = S // P
+NH = B * H
+NU = NH * NJ
+LAG = 3
+
+BF16 = mybir.dt.bfloat16
+F32 = mybir.dt.float32
+U32 = mybir.dt.uint32
+U8 = mybir.dt.uint8
+FP8X4 = mybir.dt.float8_e4m3fn_x4
+SILU = mybir.ActivationFunctionType.Silu
+
+T_FIRST = [0, 0, 0, 3, 6, 8, 11, 14, 16]
+
+
+def tile_pointwisespaggregatedattention_kernel(tc, v, k, q, out):
+    nc = tc.nc
+    with ExitStack() as ctx:
+        const = ctx.enter_context(tc.tile_pool(name="const", bufs=1))
+        inputs = ctx.enter_context(tc.tile_pool(name="inputs", bufs=1))
+        heads = ctx.enter_context(tc.tile_pool(name="heads", bufs=2))
+        units = ctx.enter_context(tc.tile_pool(name="units", bufs=4))
+        ps_sc = ctx.enter_context(tc.psum_pool(name="ps_sc", bufs=4))
+        ps_tp = ctx.enter_context(tc.psum_pool(name="ps_tp", bufs=2))
+        ps_ob = ctx.enter_context(tc.psum_pool(name="ps_ob", bufs=2))
+        ctx.enter_context(tc.manual_schedule())
+
+        k_rows = k.rearrange("b (g p t) c -> b g p t c", g=G, p=P, t=PACK)
+        v_rows = v.rearrange("b (g p t) c -> b g p t c", g=G, p=P, t=PACK)
+        q_rows = q.rearrange("b (m j) c -> b m j c", j=NJ)
+        o_rows = out.rearrange("b (m j) c -> b m j c", j=NJ)
+
+        ident = const.tile([P, P], BF16, name="ident")
+        make_identity(nc, ident[:])
+
+        k_in = {}
+        q_in = {}
+        v_in = {}
+
+        def load_head(hh):
+            b, h = divmod(hh, H)
+            cols = slice(h * HD, (h + 1) * HD)
+            for g in range(G):
+                k_tile = inputs.tile([P, PACK, HD], BF16, name="k_%d_%d" % (hh, g))
+                nc.sync.dma_start(out=k_tile[:], in_=k_rows[b, g, :, :, cols])
+                k_in[(hh, g)] = k_tile
+                q_tile = inputs.tile([P, PACK, HD], BF16, name="q_%d_%d" % (hh, g))
+                nc.sync.dma_start(out=q_tile[:], in_=q_rows[b, :, PACK * g : PACK * (g + 1), cols])
+                q_in[(hh, g)] = q_tile
+            v_tile = inputs.tile([P, G, PACK, HD], BF16, name="v_%d" % hh)
+            for g in range(G):
+                nc.sync.dma_start(out=v_tile[:, g], in_=v_rows[b, g, :, :, cols])
+            v_in[hh] = v_tile
+
+        load_head(0)
+        load_head(1)
+
+        kT = {}
+        qT = {}
+        v_grouped = {}
+        v_codes = {}
+        v_scales = {}
+        banks = {}
+        p_grouped = {}
+        p_codes = {}
+        p_scales = {}
+        o_bank = {}
+        t_bank = {}
+
+        def transpose_job(hh, n):
+            src = k_in if n < G * PACK else q_in
+            half, r = divmod(n % (G * PACK), PACK)
+            nc.tensor.transpose(
+                out=t_bank[(hh, n // 8)][:, n % 8, :], in_=src[(hh, half)][:, r, :], identity=ident[:]
+            )
+
+        def regroup_v(hh):
+            vg = heads.tile([P, G, HD, PACK], BF16, name="vg", align_bytes=64)
+            nc.vector.tensor_copy(out=vg[:], in_=v_in[hh].rearrange("p g t d -> p g d t"))
+            v_grouped[hh] = vg
+
+        def quantise_v(hh):
+            vc = heads.tile([P, G * HD], U32, name="vc", align_bytes=64)
+            vs = heads.tile([P, G * HD], U8, name="vs", align_bytes=64)
+            nc.vector.quantize_mx(
+                out=vc[:].bitcast(FP8X4),
+                scales=vs[:],
+                in_=v_grouped[hh][:].rearrange("p g d t -> p (g d t)"),
+            )
+            v_codes[hh] = vc
+            v_scales[hh] = vs
+
+        def scores(u, g):
+            hh, j = divmod(u, NJ)
+            bank = ps_sc.tile([P, PACK, P], F32, name="sc")
+            for t in range(PACK):
+                nc.tensor.matmul(
+                    out=bank[:, t, :],
+                    lhsT=kT[hh][:, g * PACK + t, :],
+                    rhs=qT[hh][:, j, :],
+                    start=True,
+                    stop=True,
+                )
+            banks[(u, g)] = bank
+
+        def silu(u):
+            pg = units.tile([P, G, P, PACK], BF16, name="pg", align_bytes=64)
+            for g in range(G):
+                nc.scalar.activation(
+                    out=pg[:, g, :, :], in_=banks[(u, g)][:].rearrange("p t m -> p m t"), func=SILU
+                )
+            p_grouped[u] = pg
+
+        def quantise_p(u):
+            pc = units.tile([P, G * P], U32, name="pc", align_bytes=64)
+            ps = units.tile([P, G * P], U8, name="ps", align_bytes=64)
+            nc.vector.quantize_mx(
+                out=pc[:].bitcast(FP8X4),
+                scales=ps[:],
+                in_=p_grouped[u][:].rearrange("p g m t -> p (g m t)"),
+            )
+            p_codes[u] = pc
+            p_scales[u] = ps
+
+        def attend(u):
+            hh = u // NJ
+            if u % 4 == 0:
+                o_bank[u // 4] = ps_ob.tile([P, 4, HD], F32, name="ob")
+            for g in range(G):
+                cs = slice(g * P, (g + 1) * P)
+                nc.tensor.matmul_mx(
+                    out=o_bank[u // 4][:, u % 4, :],
+                    lhsT=p_codes[u][:, cs].bitcast(FP8X4),
+                    lhsT_scale=p_scales[u][:, cs],
+                    rhs=v_codes[hh][:, cs].bitcast(FP8X4),
+                    rhs_scale=v_scales[hh][:, cs],
+                    start=(g == 0),
+                    stop=(g == G - 1),
+                )
+
+        def store(n):
+            hh, half = divmod(n, 2)
+            b, h = divmod(hh, H)
+            osb = units.tile([P, 4, HD], F32, name="osb")
+            nc.vector.tensor_copy(out=osb[:], in_=o_bank[n][:])
+            nc.sync.dma_start(
+                out=o_rows[b, :, 4 * half : 4 * half + 4, h * HD : (h + 1) * HD], in_=osb[:]
+            )
+
+        kT[0] = heads.tile([P, G * PACK, P], BF16, name="kT")
+        qT[0] = heads.tile([P, NJ, P], BF16, name="qT")
+        for name, pool, tag, src, dst in (
+            ("k0", ps_tp, "tp", k_in[(0, 0)], kT[0][:, 0:PACK, :]),
+            ("q0", ps_tp, "tp", q_in[(0, 0)], qT[0][:, 0:PACK, :]),
+            ("k1", ps_ob, "ob", k_in[(0, 1)], kT[0][:, PACK : 2 * PACK, :]),
+        ):
+            piece = pool.tile([P, PACK, P], BF16, name=tag)
+            for r in range(PACK):
+                nc.tensor.transpose(out=piece[:, r, :], in_=src[:, r, :], identity=ident[:])
+            nc.vector.tensor_copy(out=dst, in_=piece[:])
+        regroup_v(0)
+
+        for i in range(NU + LAG):
+            hh, sl = divmod(i, NJ)
+            if sl == 1 and hh + 2 < NH:
+                load_head(hh + 2)
+            if 0 <= i - LAG < NU:
+                attend(i - LAG)
+            if i < NU:
+                scores(i, 0)
+            if i == 1:
+                piece = ps_tp.tile([P, PACK, P], BF16, name="tp")
+                for r in range(PACK):
+                    nc.tensor.transpose(out=piece[:, r, :], in_=q_in[(0, 1)][:, r, :], identity=ident[:])
+            if hh + 1 < NH:
+                for n in range(T_FIRST[sl], T_FIRST[sl + 1]):
+                    if n % 8 == 0:
+                        t_bank[(hh + 1, n // 8)] = ps_tp.tile([P, 8, P], BF16, name="tp")
+                    transpose_job(hh + 1, n)
+            if i < NU:
+                scores(i, 1)
+                silu(i)
+            if i == 1:
+                nc.vector.tensor_copy(out=qT[0][:, PACK : 2 * PACK, :], in_=piece[:])
+                quantise_v(0)
+            if (i - LAG) % 4 == 3 and 0 <= i - LAG < NU:
+                store((i - LAG) // 4)
+            if hh + 1 < NH and sl == 4:
+                kT[hh + 1] = heads.tile([P, G * PACK, P], BF16, name="kT")
+                nc.vector.tensor_copy(out=kT[hh + 1][:], in_=t_bank[(hh + 1, 0)][:])
+            if hh + 1 < NH and sl == 5:
+                regroup_v(hh + 1)
+            if hh + 1 < NH and sl == 7:
+                qT[hh + 1] = heads.tile([P, NJ, P], BF16, name="qT")
+                nc.vector.tensor_copy(out=qT[hh + 1][:], in_=t_bank[(hh + 1, 1)][:])
+            if 0 < hh < NH and sl == 0:
+                quantise_v(hh)
+            if 0 <= i - 1 < NU:
+                quantise_p(i - 1)

@@ -4,16 +4,17 @@ import concourse.mybir as mybir
 from concourse.masks import make_identity
 
 B, S, H, HD = 2, 1024, 8, 128
-D = H * HD
 FLOPS = 2 * 2 * B * H * S * S * HD
 
 P = 128
 PACK = 4
 G = S // (P * PACK)
+NK = G * PACK
 NJ = S // P
 NH = B * H
 NU = NH * NJ
-LAG = 3
+LAG = 4
+OB = 4
 
 BF16 = mybir.dt.bfloat16
 F32 = mybir.dt.float32
@@ -49,22 +50,39 @@ def tile_pointwisespaggregatedattention_kernel(tc, v, k, q, out):
         q_in = {}
         v_in = {}
 
-        def load_head(hh):
+        def load_k(hh, g):
             b, h = divmod(hh, H)
-            cols = slice(h * HD, (h + 1) * HD)
-            for g in range(G):
-                k_tile = inputs.tile([P, PACK, HD], BF16, name="k_%d_%d" % (hh, g))
-                nc.sync.dma_start(out=k_tile[:], in_=k_rows[b, g, :, :, cols])
-                k_in[(hh, g)] = k_tile
-                q_tile = inputs.tile([P, PACK, HD], BF16, name="q_%d_%d" % (hh, g))
-                nc.sync.dma_start(out=q_tile[:], in_=q_rows[b, :, PACK * g : PACK * (g + 1), cols])
-                q_in[(hh, g)] = q_tile
-            v_tile = inputs.tile([P, G, PACK, HD], BF16, name="v_%d" % hh)
-            for g in range(G):
-                nc.sync.dma_start(out=v_tile[:, g], in_=v_rows[b, g, :, :, cols])
-            v_in[hh] = v_tile
+            tile_ = inputs.tile([P, PACK, HD], BF16, name="k_%d_%d" % (hh, g))
+            nc.sync.dma_start(out=tile_[:], in_=k_rows[b, g, :, :, h * HD : (h + 1) * HD])
+            for t in range(PACK):
+                k_in[(hh, g * PACK + t)] = tile_[:, t, :]
 
-        load_head(0)
+        def load_q(hh, j0, j1):
+            b, h = divmod(hh, H)
+            tile_ = inputs.tile([P, j1 - j0, HD], BF16, name="q_%d_%d" % (hh, j0))
+            nc.sync.dma_start(out=tile_[:], in_=q_rows[b, :, j0:j1, h * HD : (h + 1) * HD])
+            for j in range(j0, j1):
+                q_in[(hh, j)] = tile_[:, j - j0, :]
+
+        def load_v(hh):
+            b, h = divmod(hh, H)
+            tile_ = inputs.tile([P, G, PACK, HD], BF16, name="v_%d" % hh)
+            for g in range(G):
+                nc.sync.dma_start(out=tile_[:, g], in_=v_rows[b, g, :, :, h * HD : (h + 1) * HD])
+            v_in[hh] = tile_
+
+        def load_head(hh):
+            load_k(hh, 0)
+            load_k(hh, 1)
+            load_q(hh, 0, NJ)
+            load_v(hh)
+
+        load_q(0, 0, 1)
+        load_k(0, 0)
+        load_k(0, 1)
+        load_q(0, 1, 4)
+        load_q(0, 4, NJ)
+        load_v(0)
         load_head(1)
 
         kT = {}
@@ -79,12 +97,11 @@ def tile_pointwisespaggregatedattention_kernel(tc, v, k, q, out):
         o_bank = {}
         t_bank = {}
 
-        def transpose_job(hh, n):
-            src = k_in if n < G * PACK else q_in
-            half, r = divmod(n % (G * PACK), PACK)
-            nc.tensor.transpose(
-                out=t_bank[(hh, n // 8)][:, n % 8, :], in_=src[(hh, half)][:, r, :], identity=ident[:]
-            )
+        def transposes(pool, tag, width, srcs):
+            bank = pool.tile([P, width, P], BF16, name=tag)
+            for r in range(len(srcs)):
+                nc.tensor.transpose(out=bank[:, r, :], in_=srcs[r], identity=ident[:])
+            return bank
 
         def regroup_v(hh):
             vg = heads.tile([P, G, HD, PACK], BF16, name="vg", align_bytes=64)
@@ -136,12 +153,15 @@ def tile_pointwisespaggregatedattention_kernel(tc, v, k, q, out):
 
         def attend(u):
             hh = u // NJ
-            if u % 4 == 0:
-                o_bank[u // 4] = ps_ob.tile([P, 4, HD], F32, name="ob")
+            if u % OB == 0 or u == NU - 1:
+                o_bank[u] = (ps_ob.tile([P, OB, HD], F32, name="ob"), 0)
+            else:
+                o_bank[u] = (o_bank[u - 1][0], o_bank[u - 1][1] + 1)
+            bank, slot = o_bank[u]
             for g in range(G):
                 cs = slice(g * P, (g + 1) * P)
                 nc.tensor.matmul_mx(
-                    out=o_bank[u // 4][:, u % 4, :],
+                    out=bank[:, slot, :],
                     lhsT=p_codes[u][:, cs].bitcast(FP8X4),
                     lhsT_scale=p_scales[u][:, cs],
                     rhs=v_codes[hh][:, cs].bitcast(FP8X4),
@@ -150,62 +170,71 @@ def tile_pointwisespaggregatedattention_kernel(tc, v, k, q, out):
                     stop=(g == G - 1),
                 )
 
-        def store(n):
-            hh, half = divmod(n, 2)
+        def store(u, n):
+            hh, j = divmod(u, NJ)
             b, h = divmod(hh, H)
-            osb = units.tile([P, 4, HD], F32, name="osb")
-            nc.vector.tensor_copy(out=osb[:], in_=o_bank[n][:])
-            nc.sync.dma_start(
-                out=o_rows[b, :, 4 * half : 4 * half + 4, h * HD : (h + 1) * HD], in_=osb[:]
-            )
+            bank, slot = o_bank[u]
+            osb = units.tile([P, OB, HD], F32, name="osb")
+            nc.vector.tensor_copy(out=osb[:, 0:n, :], in_=bank[:, slot : slot + n, :])
+            nc.sync.dma_start(out=o_rows[b, :, j : j + n, h * HD : (h + 1) * HD], in_=osb[:, 0:n, :])
 
-        kT[0] = heads.tile([P, G * PACK, P], BF16, name="kT")
+        kT[0] = heads.tile([P, NK, P], BF16, name="kT")
         qT[0] = heads.tile([P, NJ, P], BF16, name="qT")
-        for name, pool, tag, src, dst in (
-            ("k0", ps_tp, "tp", k_in[(0, 0)], kT[0][:, 0:PACK, :]),
-            ("q0", ps_tp, "tp", q_in[(0, 0)], qT[0][:, 0:PACK, :]),
-            ("k1", ps_ob, "ob", k_in[(0, 1)], kT[0][:, PACK : 2 * PACK, :]),
-        ):
-            piece = pool.tile([P, PACK, P], BF16, name=tag)
-            for r in range(PACK):
-                nc.tensor.transpose(out=piece[:, r, :], in_=src[:, r, :], identity=ident[:])
-            nc.vector.tensor_copy(out=dst, in_=piece[:])
-        regroup_v(0)
+        piece = transposes(ps_tp, "tp", 1, [q_in[(0, 0)]])
+        nc.vector.tensor_copy(out=qT[0][:, 0:1, :], in_=piece[:])
+        piece = transposes(ps_tp, "tp", PACK, [k_in[(0, t)] for t in range(PACK)])
+        nc.vector.tensor_copy(out=kT[0][:, 0:PACK, :], in_=piece[:])
+        piece = transposes(ps_ob, "ob", PACK, [k_in[(0, t)] for t in range(PACK, NK)])
+        nc.vector.tensor_copy(out=kT[0][:, PACK:NK, :], in_=piece[:])
 
-        for i in range(NU + LAG):
+        for i in range(NU):
             hh, sl = divmod(i, NJ)
             if sl == 1 and hh + 2 < NH:
                 load_head(hh + 2)
-            if 0 <= i - LAG < NU:
+            if i >= LAG:
                 attend(i - LAG)
-            if i < NU:
-                scores(i, 0)
+            scores(i, 0)
+            if i == 0:
+                piece = transposes(ps_ob, "ob", 3, [q_in[(0, j)] for j in range(1, 4)])
             if i == 1:
-                piece = ps_tp.tile([P, PACK, P], BF16, name="tp")
-                for r in range(PACK):
-                    nc.tensor.transpose(out=piece[:, r, :], in_=q_in[(0, 1)][:, r, :], identity=ident[:])
+                piece = transposes(ps_tp, "tp", 4, [q_in[(0, j)] for j in range(4, NJ)])
             if hh + 1 < NH:
                 for n in range(T_FIRST[sl], T_FIRST[sl + 1]):
                     if n % 8 == 0:
                         t_bank[(hh + 1, n // 8)] = ps_tp.tile([P, 8, P], BF16, name="tp")
-                    transpose_job(hh + 1, n)
-            if i < NU:
-                scores(i, 1)
-                silu(i)
+                    nc.tensor.transpose(
+                        out=t_bank[(hh + 1, n // 8)][:, n % 8, :],
+                        in_=k_in[(hh + 1, n)] if n < NK else q_in[(hh + 1, n - NK)],
+                        identity=ident[:],
+                    )
+            scores(i, 1)
+            silu(i)
+            if i == 0:
+                nc.vector.tensor_copy(out=qT[0][:, 1:4, :], in_=piece[:])
+                regroup_v(0)
             if i == 1:
-                nc.vector.tensor_copy(out=qT[0][:, PACK : 2 * PACK, :], in_=piece[:])
-                quantise_v(0)
-            if (i - LAG) % 4 == 3 and 0 <= i - LAG < NU:
-                store((i - LAG) // 4)
-            if hh + 1 < NH and sl == 4:
-                kT[hh + 1] = heads.tile([P, G * PACK, P], BF16, name="kT")
-                nc.vector.tensor_copy(out=kT[hh + 1][:], in_=t_bank[(hh + 1, 0)][:])
+                nc.vector.tensor_copy(out=qT[0][:, 4:NJ, :], in_=piece[:])
+            if sl == 1:
+                quantise_v(hh)
+            if i - LAG >= OB and (i - LAG) % OB == 0:
+                store(i - LAG - OB, OB)
             if hh + 1 < NH and sl == 5:
+                kT[hh + 1] = heads.tile([P, NK, P], BF16, name="kT")
+                nc.vector.tensor_copy(out=kT[hh + 1][:], in_=t_bank[(hh + 1, 0)][:])
+            if hh + 1 < NH and sl == 6:
                 regroup_v(hh + 1)
             if hh + 1 < NH and sl == 7:
                 qT[hh + 1] = heads.tile([P, NJ, P], BF16, name="qT")
                 nc.vector.tensor_copy(out=qT[hh + 1][:], in_=t_bank[(hh + 1, 1)][:])
-            if 0 < hh < NH and sl == 0:
-                quantise_v(hh)
-            if 0 <= i - 1 < NU:
+            if i >= 1:
                 quantise_p(i - 1)
+
+        attend(NU - 4)
+        attend(NU - 3)
+        store(NU - 8, OB)
+        store(NU - 4, 2)
+        attend(NU - 2)
+        store(NU - 2, 1)
+        quantise_p(NU - 1)
+        attend(NU - 1)
+        store(NU - 1, 1)

@@ -24,6 +24,7 @@ FP8X4 = mybir.dt.float8_e4m3fn_x4
 SILU = mybir.ActivationFunctionType.Silu
 
 T_FIRST = [0, 0, 0, 3, 6, 8, 11, 14, 16]
+T_FIRST_HEAD0 = [0, 0, 0, 0, 0, 4, 8, 12, 16]
 
 
 def tile_pointwisespaggregatedattention_kernel(tc, v, k, q, out):
@@ -196,10 +197,11 @@ def tile_pointwisespaggregatedattention_kernel(tc, v, k, q, out):
             scores(i, 0)
             if i == 0:
                 piece = transposes(ps_ob, "ob", 3, [q_in[(0, j)] for j in range(1, 4)])
-            if i == 1:
+            if i == 3:
                 piece = transposes(ps_tp, "tp", 4, [q_in[(0, j)] for j in range(4, NJ)])
             if hh + 1 < NH:
-                for n in range(T_FIRST[sl], T_FIRST[sl + 1]):
+                first = T_FIRST_HEAD0 if hh == 0 else T_FIRST
+                for n in range(first[sl], first[sl + 1]):
                     if n % 8 == 0:
                         t_bank[(hh + 1, n // 8)] = ps_tp.tile([P, 8, P], BF16, name="tp")
                     nc.tensor.transpose(
@@ -212,17 +214,19 @@ def tile_pointwisespaggregatedattention_kernel(tc, v, k, q, out):
             if i == 0:
                 nc.vector.tensor_copy(out=qT[0][:, 1:4, :], in_=piece[:])
                 regroup_v(0)
-            if i == 1:
+            if i == 3:
                 nc.vector.tensor_copy(out=qT[0][:, 4:NJ, :], in_=piece[:])
             if sl == 1:
                 quantise_v(hh)
             if i - LAG >= OB and (i - LAG) % OB == 0:
                 store(i - LAG - OB, OB)
+            if i == NU - 1:
+                store(NU - 2 * OB, OB)
             if hh + 1 < NH and sl == 5:
+                regroup_v(hh + 1)
+            if hh + 1 < NH and sl == 6:
                 kT[hh + 1] = heads.tile([P, NK, P], BF16, name="kT")
                 nc.vector.tensor_copy(out=kT[hh + 1][:], in_=t_bank[(hh + 1, 0)][:])
-            if hh + 1 < NH and sl == 6:
-                regroup_v(hh + 1)
             if hh + 1 < NH and sl == 7:
                 qT[hh + 1] = heads.tile([P, NJ, P], BF16, name="qT")
                 nc.vector.tensor_copy(out=qT[hh + 1][:], in_=t_bank[(hh + 1, 1)][:])
@@ -231,10 +235,9 @@ def tile_pointwisespaggregatedattention_kernel(tc, v, k, q, out):
 
         attend(NU - 4)
         attend(NU - 3)
-        store(NU - 8, OB)
         store(NU - 4, 2)
         attend(NU - 2)
-        store(NU - 2, 1)
         quantise_p(NU - 1)
+        store(NU - 2, 1)
         attend(NU - 1)
         store(NU - 1, 1)

@@ -15,6 +15,7 @@ NH = B * H
 NU = NH * NJ
 LAG = 4
 OB = 4
+NWARM = 3
 
 BF16 = mybir.dt.bfloat16
 F32 = mybir.dt.float32
@@ -46,6 +47,12 @@ def tile_pointwisespaggregatedattention_kernel(tc, v, k, q, out):
 
         ident = const.tile([P, P], BF16, name="ident")
         make_identity(nc, ident[:])
+
+        warm = const.tile([P, 512], BF16, name="warm")
+        nc.vector.memset(warm[:], 0.0)
+        wbank = ps_sc.tile([P, 512], F32, name="sc")
+        for n in range(NWARM):
+            nc.tensor.matmul(out=wbank[:], lhsT=warm[:, 0:P], rhs=warm[:], start=True, stop=True)
 
         k_in = {}
         q_in = {}

@@ -159,14 +159,25 @@ def tile_pointwisespaggregatedattention_kernel(tc, v, k, q, out):
             p_codes[u] = pc
             p_scales[u] = ps
 
-        def attend(u):
+        def quantise_pass(u, g):
+            if g == 0:
+                p_codes[u] = units.tile([P, G * P], U32, name="pc", align_bytes=64)
+                p_scales[u] = units.tile([P, G * P], U8, name="ps", align_bytes=64)
+            cs = slice(g * P, (g + 1) * P)
+            nc.vector.quantize_mx(
+                out=p_codes[u][:, cs].bitcast(FP8X4),
+                scales=p_scales[u][:, cs],
+                in_=p_grouped[u][:, g].rearrange("p m t -> p (m t)"),
+            )
+
+        def attend(u, passes=(0, 1)):
             hh = u // NJ
-            if u % OB == 0 or u == NU - 1:
+            if passes[0] == 0 and (u % OB == 0 or u == NU - 1):
                 o_bank[u] = (ps_ob.tile([P, OB, HD], F32, name="ob"), 0)
-            else:
+            elif passes[0] == 0:
                 o_bank[u] = (o_bank[u - 1][0], o_bank[u - 1][1] + 1)
             bank, slot = o_bank[u]
-            for g in range(G):
+            for g in passes:
                 cs = slice(g * P, (g + 1) * P)
                 nc.tensor.matmul_mx(
                     out=bank[:, slot, :],
@@ -244,7 +255,9 @@ def tile_pointwisespaggregatedattention_kernel(tc, v, k, q, out):
         attend(NU - 3)
         store(NU - 4, 2)
         attend(NU - 2)
-        quantise_p(NU - 1)
+        quantise_pass(NU - 1, 0)
+        attend(NU - 1, (0,))
+        quantise_pass(NU - 1, 1)
+        attend(NU - 1, (1,))
         store(NU - 2, 1)
-        attend(NU - 1)
         store(NU - 1, 1)

from contextlib import ExitStack

import concourse.mybir as mybir
from concourse.masks import make_identity

B, S, H, HD = 2, 1024, 8, 128
FLOPS = 2 * 2 * B * H * S * S * HD

P = 128
PACK = 4
G = S // (P * PACK)
NK = G * PACK
NJ = S // P
NH = B * H
NU = NH * NJ
LAG = 4
OB = 4
NWARM = 3

BF16 = mybir.dt.bfloat16
F32 = mybir.dt.float32
U32 = mybir.dt.uint32
U8 = mybir.dt.uint8
FP8X4 = mybir.dt.float8_e4m3fn_x4
SILU = mybir.ActivationFunctionType.Silu

T_FIRST = [0, 0, 0, 3, 6, 8, 11, 14, 16]
T_FIRST_HEAD0 = [0, 0, 0, 0, 0, 4, 8, 12, 16]


def tile_pointwisespaggregatedattention_kernel(tc, v, k, q, out):
    nc = tc.nc
    with ExitStack() as ctx:
        const = ctx.enter_context(tc.tile_pool(name="const", bufs=1))
        inputs = ctx.enter_context(tc.tile_pool(name="inputs", bufs=1))
        heads = ctx.enter_context(tc.tile_pool(name="heads", bufs=2))
        units = ctx.enter_context(tc.tile_pool(name="units", bufs=4))
        ps_sc = ctx.enter_context(tc.psum_pool(name="ps_sc", bufs=4))
        ps_tp = ctx.enter_context(tc.psum_pool(name="ps_tp", bufs=2))
        ps_ob = ctx.enter_context(tc.psum_pool(name="ps_ob", bufs=2))
        ctx.enter_context(tc.manual_schedule())

        k_rows = k.rearrange("b (g p t) c -> b g p t c", g=G, p=P, t=PACK)
        v_rows = v.rearrange("b (g p t) c -> b g p t c", g=G, p=P, t=PACK)
        q_rows = q.rearrange("b (m j) c -> b m j c", j=NJ)
        o_rows = out.rearrange("b (m j) c -> b m j c", j=NJ)

        ident = const.tile([P, P], BF16, name="ident")
        make_identity(nc, ident[:])

        warm = const.tile([P, 512], BF16, name="warm")
        nc.vector.memset(warm[:], 0.0)
        wbank = ps_sc.tile([P, 512], F32, name="sc")
        for n in range(NWARM):
            nc.tensor.matmul(out=wbank[:], lhsT=warm[:, 0:P], rhs=warm[:], start=True, stop=True)

        k_in = {}
        q_in = {}
        v_in = {}

        def load_k(hh, g):
            b, h = divmod(hh, H)
            tile_ = inputs.tile([P, PACK, HD], BF16, name="k_%d_%d" % (hh, g))
            nc.sync.dma_start(out=tile_[:], in_=k_rows[b, g, :, :, h * HD : (h + 1) * HD])
            for t in range(PACK):
                k_in[(hh, g * PACK + t)] = tile_[:, t, :]

        def load_q(hh, j0, j1):
            b, h = divmod(hh, H)
            tile_ = inputs.tile([P, j1 - j0, HD], BF16, name="q_%d_%d" % (hh, j0))
            nc.sync.dma_start(out=tile_[:], in_=q_rows[b, :, j0:j1, h * HD : (h + 1) * HD])
            for j in range(j0, j1):
                q_in[(hh, j)] = tile_[:, j - j0, :]

        def load_v(hh):
            b, h = divmod(hh, H)
            tile_ = inputs.tile([P, G, PACK, HD], BF16, name="v_%d" % hh)
            for g in range(G):
                nc.sync.dma_start(out=tile_[:, g], in_=v_rows[b, g, :, :, h * HD : (h + 1) * HD])
            v_in[hh] = tile_

        def load_head(hh):
            load_k(hh, 0)
            load_k(hh, 1)
            load_q(hh, 0, NJ)
            load_v(hh)

        load_q(0, 0, 1)
        load_k(0, 0)
        load_k(0, 1)
        load_q(0, 1, 4)
        load_q(0, 4, NJ)
        load_v(0)
        load_head(1)

        kT = {}
        qT = {}
        v_grouped = {}
        v_codes = {}
        v_scales = {}
        banks = {}
        p_grouped = {}
        p_codes = {}
        p_scales = {}
        o_bank = {}
        t_bank = {}

        def transposes(pool, tag, width, srcs):
            bank = pool.tile([P, width, P], BF16, name=tag)
            for r in range(len(srcs)):
                nc.tensor.transpose(out=bank[:, r, :], in_=srcs[r], identity=ident[:])
            return bank

        def regroup_v(hh):
            vg = heads.tile([P, G, HD, PACK], BF16, name="vg", align_bytes=64)
            nc.vector.tensor_copy(out=vg[:], in_=v_in[hh].rearrange("p g t d -> p g d t"))
            v_grouped[hh] = vg

        def quantise_v(hh):
            vc = heads.tile([P, G * HD], U32, name="vc", align_bytes=64)
            vs = heads.tile([P, G * HD], U8, name="vs", align_bytes=64)
            nc.vector.quantize_mx(
                out=vc[:].bitcast(FP8X4),
                scales=vs[:],
                in_=v_grouped[hh][:].rearrange("p g d t -> p (g d t)"),
            )
            v_codes[hh] = vc
            v_scales[hh] = vs

        def scores(u, g):
            hh, j = divmod(u, NJ)
            bank = ps_sc.tile([P, PACK, P], F32, name="sc")
            for t in range(PACK):
                nc.tensor.matmul(
                    out=bank[:, t, :],
                    lhsT=kT[hh][:, g * PACK + t, :],
                    rhs=qT[hh][:, j, :],
                    start=True,
                    stop=True,
                )
            banks[(u, g)] = bank

        def silu(u):
            pg = units.tile([P, G, P, PACK], BF16, name="pg", align_bytes=64)
            for g in range(G):
                nc.scalar.activation(
                    out=pg[:, g, :, :], in_=banks[(u, g)][:].rearrange("p t m -> p m t"), func=SILU
                )
            p_grouped[u] = pg

        def quantise_p(u):
            pc = units.tile([P, G * P], U32, name="pc", align_bytes=64)
            ps = units.tile([P, G * P], U8, name="ps", align_bytes=64)
            nc.vector.quantize_mx(
                out=pc[:].bitcast(FP8X4),
                scales=ps[:],
                in_=p_grouped[u][:].rearrange("p g m t -> p (g m t)"),
            )
            p_codes[u] = pc
            p_scales[u] = ps

        def quantise_pass(u, g):
            if g == 0:
                p_codes[u] = units.tile([P, G * P], U32, name="pc", align_bytes=64)
                p_scales[u] = units.tile([P, G * P], U8, name="ps", align_bytes=64)
            cs = slice(g * P, (g + 1) * P)
            nc.vector.quantize_mx(
                out=p_codes[u][:, cs].bitcast(FP8X4),
                scales=p_scales[u][:, cs],
                in_=p_grouped[u][:, g].rearrange("p m t -> p (m t)"),
            )

        def attend(u, passes=(0, 1)):
            hh = u // NJ
            if passes[0] == 0 and (u % OB == 0 or u == NU - 1):
                o_bank[u] = (ps_ob.tile([P, OB, HD], F32, name="ob"), 0)
            elif passes[0] == 0:
                o_bank[u] = (o_bank[u - 1][0], o_bank[u - 1][1] + 1)
            bank, slot = o_bank[u]
            for g in passes:
                cs = slice(g * P, (g + 1) * P)
                nc.tensor.matmul_mx(
                    out=bank[:, slot, :],
                    lhsT=p_codes[u][:, cs].bitcast(FP8X4),
                    lhsT_scale=p_scales[u][:, cs],
                    rhs=v_codes[hh][:, cs].bitcast(FP8X4),
                    rhs_scale=v_scales[hh][:, cs],
                    start=(g == 0),
                    stop=(g == G - 1),
                )

        def store(u, n):
            hh, j = divmod(u, NJ)
            b, h = divmod(hh, H)
            bank, slot = o_bank[u]
            osb = units.tile([P, OB, HD], F32, name="osb")
            nc.vector.tensor_copy(out=osb[:, 0:n, :], in_=bank[:, slot : slot + n, :])
            nc.sync.dma_start(out=o_rows[b, :, j : j + n, h * HD : (h + 1) * HD], in_=osb[:, 0:n, :])

        kT[0] = heads.tile([P, NK, P], BF16, name="kT")
        qT[0] = heads.tile([P, NJ, P], BF16, name="qT")
        piece = transposes(ps_tp, "tp", 1, [q_in[(0, 0)]])
        nc.vector.tensor_copy(out=qT[0][:, 0:1, :], in_=piece[:])
        piece = transposes(ps_tp, "tp", PACK, [k_in[(0, t)] for t in range(PACK)])
        nc.vector.tensor_copy(out=kT[0][:, 0:PACK, :], in_=piece[:])
        piece = transposes(ps_ob, "ob", PACK, [k_in[(0, t)] for t in range(PACK, NK)])
        nc.vector.tensor_copy(out=kT[0][:, PACK:NK, :], in_=piece[:])

        for i in range(NU):
            hh, sl = divmod(i, NJ)
            if sl == 1 and hh + 2 < NH:
                load_head(hh + 2)
            if i >= LAG:
                attend(i - LAG)
            scores(i, 0)
            if i == 0:
                piece = transposes(ps_ob, "ob", 3, [q_in[(0, j)] for j in range(1, 4)])
            if i == 3:
                piece = transposes(ps_tp, "tp", 4, [q_in[(0, j)] for j in range(4, NJ)])
            if hh + 1 < NH:
                first = T_FIRST_HEAD0 if hh == 0 else T_FIRST
                for n in range(first[sl], first[sl + 1]):
                    if n % 8 == 0:
                        t_bank[(hh + 1, n // 8)] = ps_tp.tile([P, 8, P], BF16, name="tp")
                    nc.tensor.transpose(
                        out=t_bank[(hh + 1, n // 8)][:, n % 8, :],
                        in_=k_in[(hh + 1, n)] if n < NK else q_in[(hh + 1, n - NK)],
                        identity=ident[:],
                    )
            scores(i, 1)
            silu(i)
            if i == 0:
                nc.vector.tensor_copy(out=qT[0][:, 1:4, :], in_=piece[:])
                regroup_v(0)
            if i == 3:
                nc.vector.tensor_copy(out=qT[0][:, 4:NJ, :], in_=piece[:])
            if sl == 1:
                quantise_v(hh)
            if i - LAG >= OB and (i - LAG) % OB == 0:
                store(i - LAG - OB, OB)
            if i == NU - 1:
                store(NU - 2 * OB, OB)
            if hh + 1 < NH and sl == 5:
                regroup_v(hh + 1)
            if hh + 1 < NH and sl == 6:
                kT[hh + 1] = heads.tile([P, NK, P], BF16, name="kT")
                nc.vector.tensor_copy(out=kT[hh + 1][:], in_=t_bank[(hh + 1, 0)][:])
            if hh + 1 < NH and sl == 7:
                qT[hh + 1] = heads.tile([P, NJ, P], BF16, name="qT")
                nc.vector.tensor_copy(out=qT[hh + 1][:], in_=t_bank[(hh + 1, 1)][:])
            if i >= 1:
                quantise_p(i - 1)

        attend(NU - 4)
        attend(NU - 3)
        store(NU - 4, 2)
        attend(NU - 2)
        quantise_pass(NU - 1, 0)
        attend(NU - 1, (0,))
        quantise_pass(NU - 1, 1)
        attend(NU - 1, (1,))
        store(NU - 2, 1)
        store(NU - 1, 1)
